import numpy as np
import ml_dtypes


def mxq(x, axis, fmt="e4m3"):
    dtype, down = {"e4m3": (ml_dtypes.float8_e4m3fn, 7), "e5m2": (ml_dtypes.float8_e5m2, 14)}[fmt]
    v = np.moveaxis(np.asarray(x, np.float32).astype(ml_dtypes.bfloat16).astype(np.float64), axis, -1)
    blocks = v.reshape(v.shape[:-1] + (-1, 32))
    amax = np.abs(blocks).max(-1, keepdims=True)
    byte = np.maximum(np.where(amax > 0, np.frexp(amax)[1] - 1 + 127, 0) - down, 1)
    scale = np.exp2(byte - 127.0)
    codes = (blocks / scale).astype(np.float32).astype(dtype).astype(np.float64)
    return np.moveaxis((codes * scale).reshape(v.shape), -1, axis)


WIDE = False


def mx_kscale(k):
    if not WIDE:
        return np.ones(k)
    levels = np.array([10, -10, 5, -5, 0])
    a = np.random.permutation(np.resize(levels, k // 512 * 4)).reshape(k // 512, 4)
    idx = np.arange(k)
    return np.exp2(a[idx // 512, idx % 128 // 32])


BF16 = ml_dtypes.bfloat16


def bf(x):
    return np.asarray(x, np.float32).astype(BF16)


def f64(x):
    return np.asarray(x).astype(np.float64)


E2M1 = np.array([0.0, 0.5, 1.0, 1.5, 2.0, 3.0, 4.0, 6.0, -0.0, -0.5, -1.0, -1.5, -2.0, -3.0, -4.0, -6.0])


def pack_weight(w, fmt):
    k, n = w.shape
    w = f64(bf(w)).reshape(k // 32, 32, n)
    amax = np.abs(w).max(1)
    if fmt == "e4m3":
        byte = np.frexp(amax)[1] - 1 + 127 - 7
    else:
        mant, ex = np.frexp(amax / 6.0)
        byte = np.where(mant > 0.5, ex, ex - 1) + 127
    byte = np.clip(np.where(amax > 0, byte, 1), 1, 254)
    scaled = (w * np.exp2(127.0 - byte)[:, None, :]).reshape(k, n).astype(np.float32)
    by_word = np.ascontiguousarray(scaled.reshape(k // 512, 128, 4, n).transpose(0, 1, 3, 2))
    if fmt == "e4m3":
        words = by_word.astype(ml_dtypes.float8_e4m3fn).view(np.uint8)
    else:
        c = by_word.astype(ml_dtypes.float4_e2m1fn).view(np.uint8) & 0xF
        words = c[..., 0::2] | (c[..., 1::2] << 4)
    return np.ascontiguousarray(words), np.ascontiguousarray(byte.astype(np.uint8).reshape(k // 512, 16, n))


def unpack_weight(words, scales, fmt):
    g, p, n, _ = words.shape
    if fmt == "e4m3":
        vals = np.ascontiguousarray(words).view(ml_dtypes.float8_e4m3fn).astype(np.float64)
    else:
        nib = np.empty((g, p, n, 4), np.uint8)
        nib[..., 0::2] = words & 0xF
        nib[..., 1::2] = words >> 4
        vals = E2M1[nib]
    vals = vals * np.repeat(np.exp2(scales.astype(np.float64) - 127.0), 8, axis=1)[..., None]
    return vals.transpose(0, 1, 3, 2).reshape(g * 512, n)


B, D, K = 5120, 512, 2


def setup_inputs():
    s = mx_kscale(D)
    x = np.random.standard_normal((B, D, K)) * s[None, :, None]
    mu = np.random.standard_normal((D, K)) * 0.3 * s[:, None]
    w = (np.eye(D)[None] + np.random.standard_normal((K, D, D)) * 0.7 / np.sqrt(D)) / s[None, None, :]
    cat = np.ascontiguousarray(w.swapaxes(1, 2)).reshape(-1, D)
    words, scales = pack_weight(cat, "e4m3")
    return {"x": bf(x), "mu_track": bf(mu), "Std_inv_track_words": words, "Std_inv_track_scales": scales}


def reference(x, mu_track, Std_inv_track_words, Std_inv_track_scales):
    x_cnt = f64(x) - f64(mu_track)[None]
    xq = mxq(x_cnt, 1, "e4m3")
    wq = unpack_weight(Std_inv_track_words, Std_inv_track_scales, "e4m3").reshape(K, D, D).swapaxes(1, 2)
    z = wq @ xq.transpose(2, 1, 0)
    return z.transpose(2, 1, 0)

@@ -1,0 +1,152 @@
+from contextlib import ExitStack
+
+import concourse.mybir as mybir
+from concourse.masks import make_identity
+
+F32 = mybir.dt.float32
+BF16 = mybir.dt.bfloat16
+I32 = mybir.dt.int32
+U32 = mybir.dt.uint32
+U8 = mybir.dt.uint8
+FP8X4 = mybir.dt.float8_e4m3fn_x4
+
+P = 128
+PACK = 4
+BATCH, FEAT, CLUSTERS = 5120, 512, 2
+ROW = FEAT * CLUSTERS
+N_TILES = BATCH // P
+RUN = 2
+N_RUNS = N_TILES // RUN
+D_HALF = FEAT // 2
+SCALE_ROWS = 4
+OUT_BUFS = 12
+
+FLOPS = 2 * BATCH * FEAT * FEAT * CLUSTERS
+
+
+def tile_clusternorm1dv3_t_e_kernel(
+    tc, x, mu_track, Std_inv_track_words, Std_inv_track_scales, out
+):
+    nc = tc.nc
+    x_rows = x.rearrange("(p j) e c -> p j (e c)", j=N_TILES)
+    out_rows = out.rearrange("(p j) d c -> p j (d c)", j=N_TILES)
+
+    with ExitStack() as ctx:
+        ctx.enter_context(tc.manual_schedule())
+        const = ctx.enter_context(tc.tile_pool(name="const", bufs=1))
+        x_pool = ctx.enter_context(tc.tile_pool(name="x", bufs=N_RUNS))
+        grouped_pool = ctx.enter_context(tc.tile_pool(name="grouped", bufs=4))
+        quant_pool = ctx.enter_context(tc.tile_pool(name="quant", bufs=6))
+        out_pool = ctx.enter_context(tc.tile_pool(name="out", bufs=OUT_BUFS))
+        xt_pool = ctx.enter_context(tc.psum_pool(name="xt", bufs=2 * RUN))
+        acc_pool = ctx.enter_context(tc.psum_pool(name="acc", bufs=2 * RUN))
+
+        ident = const.tile([P, P], F32)
+        make_identity(nc, ident[:])
+
+        mu_sb = const.tile([P, PACK * CLUSTERS], BF16)
+        nc.sync.dma_start(out=mu_sb[:], in_=mu_track.rearrange("(p t) c -> p (t c)", t=PACK))
+
+        x_tiles = []
+        for r in range(N_RUNS):
+            x_sb = x_pool.tile([P, RUN, ROW], BF16)
+            x_tiles.append(x_sb)
+        nc.sync.dma_start(out=x_tiles[0][:], in_=x_rows[:, 0:RUN, :])
+
+        w_scales = const.tile([P, CLUSTERS, FEAT], U8, align_bytes=64)
+        nc.vector.memset(w_scales[:].bitcast(I32), 0)
+        for quadrant in range(P // 32):
+            nc.sync.dma_start(
+                out=w_scales[32 * quadrant : 32 * quadrant + SCALE_ROWS, :, :].bitcast(I32),
+                in_=Std_inv_track_scales[
+                    :, SCALE_ROWS * quadrant : SCALE_ROWS * (quadrant + 1), :
+                ]
+                .rearrange("c q d -> q c d")
+                .bitcast(I32),
+            )
+        w_codes = const.tile([P, CLUSTERS, FEAT], U32, align_bytes=64)
+        nc.sync.dma_start(
+            out=w_codes[:].bitcast(I32),
+            in_=Std_inv_track_words.rearrange("c p d t -> p c (d t)").bitcast(I32),
+        )
+        for r in range(1, N_RUNS):
+            nc.sync.dma_start(out=x_tiles[r][:], in_=x_rows[:, r * RUN : (r + 1) * RUN, :])
+
+        mu_spread = (
+            mu_sb[:]
+            .rearrange("p (t c) -> p c t", c=CLUSTERS)
+            .unsqueeze(2)
+            .to_broadcast([P, CLUSTERS, P, PACK])
+        )
+
+        xt_of = {}
+        grouped_of = {}
+        quant_of = {}
+
+        def transpose_run(r):
+            for j in range(r * RUN, (r + 1) * RUN):
+                words = x_tiles[r][:, j - r * RUN, :].bitcast(F32)
+                xt = xt_pool.tile([P, PACK, P], F32)
+                for t in range(PACK):
+                    nc.tensor.transpose(xt[:, t, :], words[:, t:FEAT:PACK], ident[:])
+                xt_of[j] = xt
+
+        def centre(j):
+            xt = xt_of[j]
+            grouped = grouped_pool.tile([P, CLUSTERS, P, PACK], BF16, align_bytes=64)
+            nc.vector.tensor_tensor(
+                out=grouped[:],
+                in0=xt[:].bitcast(BF16).rearrange("p t (b c) -> p c b t", c=CLUSTERS),
+                in1=mu_spread,
+                op=mybir.AluOpType.subtract,
+            )
+            grouped_of[j] = grouped
+
+        def quantise(j):
+            grouped = grouped_of[j]
+            codes = quant_pool.tile([P, CLUSTERS * P], U32, align_bytes=64)
+            scales = quant_pool.tile([P, CLUSTERS * P], U8, align_bytes=64)
+            nc.vector.quantize_mx(
+                out=codes[:].bitcast(FP8X4),
+                scales=scales[:],
+                in_=grouped[:].rearrange("p c b t -> p (c b t)"),
+            )
+            quant_of[j] = (codes, scales)
+
+        def multiply_run(r):
+            out_sb = out_pool.tile([P, RUN, ROW], F32)
+            for j in range(r * RUN, (r + 1) * RUN):
+                codes, scales = quant_of[j]
+                for half in range(FEAT // D_HALF):
+                    d_cols = slice(half * D_HALF, (half + 1) * D_HALF)
+                    acc = acc_pool.tile([P, CLUSTERS, D_HALF], F32)
+                    for c in range(CLUSTERS):
+                        b_cols = slice(c * P, (c + 1) * P)
+                        nc.tensor.matmul_mx(
+                            out=acc[:, c, :],
+                            lhsT=codes[:, b_cols].bitcast(FP8X4),
+                            lhsT_scale=scales[:, b_cols],
+                            rhs=w_codes[:, c, d_cols].bitcast(FP8X4),
+                            rhs_scale=w_scales[:, c, d_cols],
+                            start=True,
+                            stop=True,
+                        )
+                    nc.scalar.copy(
+                        out=out_sb[
+                            :, j - r * RUN, half * D_HALF * CLUSTERS : (half + 1) * D_HALF * CLUSTERS
+                        ].rearrange("p (d c) -> p d c", c=CLUSTERS),
+                        in_=acc[:].rearrange("p c d -> p d c"),
+                    )
+            nc.sync.dma_start(out=out_rows[:, r * RUN : (r + 1) * RUN, :], in_=out_sb[:])
+
+        transpose_run(0)
+        for r in range(N_RUNS + 1):
+            if r + 1 < N_RUNS:
+                transpose_run(r + 1)
+            for j in range(r * RUN, (r + 1) * RUN):
+                if j < N_TILES:
+                    centre(j)
+                if 0 <= j - 1 < N_TILES:
+                    quantise(j - 1)
+            if r >= 1:
+                multiply_run(r - 1)

@@ -19,7 +19,9 @@ RUN = 2
 N_RUNS = N_TILES // RUN
 D_HALF = FEAT // 2
 SCALE_ROWS = 4
-OUT_BUFS = 12
+LOAD_RUNS = 4
+STORE_RUNS = 2
+OUT_BUFS = 7
 
 FLOPS = 2 * BATCH * FEAT * FEAT * CLUSTERS
 
@@ -34,7 +36,7 @@ def tile_clusternorm1dv3_t_e_kernel(
     with ExitStack() as ctx:
         ctx.enter_context(tc.manual_schedule())
         const = ctx.enter_context(tc.tile_pool(name="const", bufs=1))
-        x_pool = ctx.enter_context(tc.tile_pool(name="x", bufs=N_RUNS))
+        x_pool = ctx.enter_context(tc.tile_pool(name="x", bufs=N_RUNS // LOAD_RUNS))
         grouped_pool = ctx.enter_context(tc.tile_pool(name="grouped", bufs=4))
         quant_pool = ctx.enter_context(tc.tile_pool(name="quant", bufs=6))
         out_pool = ctx.enter_context(tc.tile_pool(name="out", bufs=OUT_BUFS))
@@ -47,11 +49,19 @@ def tile_clusternorm1dv3_t_e_kernel(
         mu_sb = const.tile([P, PACK * CLUSTERS], BF16)
         nc.sync.dma_start(out=mu_sb[:], in_=mu_track.rearrange("(p t) c -> p (t c)", t=PACK))
 
-        x_tiles = []
-        for r in range(N_RUNS):
-            x_sb = x_pool.tile([P, RUN, ROW], BF16)
-            x_tiles.append(x_sb)
-        nc.sync.dma_start(out=x_tiles[0][:], in_=x_rows[:, 0:RUN, :])
+        x_blocks = []
+        for block in range(N_RUNS // LOAD_RUNS):
+            x_sb = x_pool.tile([P, LOAD_RUNS * RUN, ROW], BF16)
+            x_blocks.append(x_sb)
+
+        def load_runs(first_run, n_runs):
+            first = (first_run % LOAD_RUNS) * RUN
+            nc.sync.dma_start(
+                out=x_blocks[first_run // LOAD_RUNS][:, first : first + n_runs * RUN, :],
+                in_=x_rows[:, first_run * RUN : (first_run + n_runs) * RUN, :],
+            )
+
+        load_runs(0, 1)
 
         w_scales = const.tile([P, CLUSTERS, FEAT], U8, align_bytes=64)
         nc.vector.memset(w_scales[:].bitcast(I32), 0)
@@ -69,8 +79,10 @@ def tile_clusternorm1dv3_t_e_kernel(
             out=w_codes[:].bitcast(I32),
             in_=Std_inv_track_words.rearrange("c p d t -> p c (d t)").bitcast(I32),
         )
-        for r in range(1, N_RUNS):
-            nc.sync.dma_start(out=x_tiles[r][:], in_=x_rows[:, r * RUN : (r + 1) * RUN, :])
+        for r in range(1, LOAD_RUNS):
+            load_runs(r, 1)
+        for r in range(LOAD_RUNS, N_RUNS, LOAD_RUNS):
+            load_runs(r, LOAD_RUNS)
 
         mu_spread = (
             mu_sb[:]
@@ -82,10 +94,11 @@ def tile_clusternorm1dv3_t_e_kernel(
         xt_of = {}
         grouped_of = {}
         quant_of = {}
+        out_of = {}
 
         def transpose_run(r):
             for j in range(r * RUN, (r + 1) * RUN):
-                words = x_tiles[r][:, j - r * RUN, :].bitcast(F32)
+                words = x_blocks[r // LOAD_RUNS][:, j % (LOAD_RUNS * RUN), :].bitcast(F32)
                 xt = xt_pool.tile([P, PACK, P], F32)
                 for t in range(PACK):
                     nc.tensor.transpose(xt[:, t, :], words[:, t:FEAT:PACK], ident[:])
@@ -114,8 +127,13 @@ def tile_clusternorm1dv3_t_e_kernel(
             quant_of[j] = (codes, scales)
 
         def multiply_run(r):
-            out_sb = out_pool.tile([P, RUN, ROW], F32)
+            block = r // STORE_RUNS
+            if r % STORE_RUNS == 0:
+                out_new = out_pool.tile([P, STORE_RUNS * RUN, ROW], F32)
+                out_of[block] = out_new
+            out_sb = out_of[block]
             for j in range(r * RUN, (r + 1) * RUN):
+                row = j % (STORE_RUNS * RUN)
                 codes, scales = quant_of[j]
                 for half in range(FEAT // D_HALF):
                     d_cols = slice(half * D_HALF, (half + 1) * D_HALF)
@@ -133,11 +151,21 @@ def tile_clusternorm1dv3_t_e_kernel(
                         )
                     nc.scalar.copy(
                         out=out_sb[
-                            :, j - r * RUN, half * D_HALF * CLUSTERS : (half + 1) * D_HALF * CLUSTERS
+                            :, row, half * D_HALF * CLUSTERS : (half + 1) * D_HALF * CLUSTERS
                         ].rearrange("p (d c) -> p d c", c=CLUSTERS),
                         in_=acc[:].rearrange("p c d -> p d c"),
                     )
-            nc.sync.dma_start(out=out_rows[:, r * RUN : (r + 1) * RUN, :], in_=out_sb[:])
+            if block == N_RUNS // STORE_RUNS - 1:
+                first = (r % STORE_RUNS) * RUN
+                nc.sync.dma_start(
+                    out=out_rows[:, r * RUN : (r + 1) * RUN, :],
+                    in_=out_sb[:, first : first + RUN, :],
+                )
+            elif r % STORE_RUNS == STORE_RUNS - 1:
+                nc.sync.dma_start(
+                    out=out_rows[:, block * STORE_RUNS * RUN : (block + 1) * STORE_RUNS * RUN, :],
+                    in_=out_sb[:],
+                )
 
         transpose_run(0)
         for r in range(N_RUNS + 1):

@@ -22,6 +22,8 @@ SCALE_ROWS = 4
 LOAD_RUNS = 4
 STORE_RUNS = 2
 OUT_BUFS = 7
+SHARED_EVERY = 7
+SHARED_PHASE = 3
 
 FLOPS = 2 * BATCH * FEAT * FEAT * CLUSTERS
 
@@ -38,6 +40,7 @@ def tile_clusternorm1dv3_t_e_kernel(
         const = ctx.enter_context(tc.tile_pool(name="const", bufs=1))
         x_pool = ctx.enter_context(tc.tile_pool(name="x", bufs=N_RUNS // LOAD_RUNS))
         grouped_pool = ctx.enter_context(tc.tile_pool(name="grouped", bufs=4))
+        raw_pool = ctx.enter_context(tc.tile_pool(name="raw", bufs=2))
         quant_pool = ctx.enter_context(tc.tile_pool(name="quant", bufs=6))
         out_pool = ctx.enter_context(tc.tile_pool(name="out", bufs=OUT_BUFS))
         xt_pool = ctx.enter_context(tc.psum_pool(name="xt", bufs=2 * RUN))
@@ -91,6 +94,13 @@ def tile_clusternorm1dv3_t_e_kernel(
             .to_broadcast([P, CLUSTERS, P, PACK])
         )
 
+        mu_full = const.tile([P, CLUSTERS, P, PACK], BF16)
+        nc.vector.tensor_copy(out=mu_full[:], in_=mu_spread)
+
+        def shared(j):
+            return j % SHARED_EVERY == SHARED_PHASE
+
+        raw_of = {}
         xt_of = {}
         grouped_of = {}
         quant_of = {}
@@ -103,16 +113,27 @@ def tile_clusternorm1dv3_t_e_kernel(
                 for t in range(PACK):
                     nc.tensor.transpose(xt[:, t, :], words[:, t:FEAT:PACK], ident[:])
                 xt_of[j] = xt
+                if shared(j):
+                    raw = raw_pool.tile([P, CLUSTERS, P, PACK], BF16)
+                    nc.scalar.copy(
+                        out=raw[:],
+                        in_=xt[:].bitcast(BF16).rearrange("p t (b c) -> p c b t", c=CLUSTERS),
+                    )
+                    raw_of[j] = raw
 
         def centre(j):
-            xt = xt_of[j]
             grouped = grouped_pool.tile([P, CLUSTERS, P, PACK], BF16, align_bytes=64)
-            nc.vector.tensor_tensor(
-                out=grouped[:],
-                in0=xt[:].bitcast(BF16).rearrange("p t (b c) -> p c b t", c=CLUSTERS),
-                in1=mu_spread,
-                op=mybir.AluOpType.subtract,
-            )
+            if shared(j):
+                nc.vector.tensor_tensor(
+                    out=grouped[:], in0=raw_of[j][:], in1=mu_full[:], op=mybir.AluOpType.subtract
+                )
+            else:
+                nc.vector.tensor_tensor(
+                    out=grouped[:],
+                    in0=xt_of[j][:].bitcast(BF16).rearrange("p t (b c) -> p c b t", c=CLUSTERS),
+                    in1=mu_spread,
+                    op=mybir.AluOpType.subtract,
+                )
             grouped_of[j] = grouped
 
         def quantise(j):

@@ -19,9 +19,9 @@ RUN = 2
 N_RUNS = N_TILES // RUN
 D_HALF = FEAT // 2
 SCALE_ROWS = 4
-LOAD_RUNS = 4
-STORE_RUNS = 2
-OUT_BUFS = 7
+LOAD_TILES = (2, 2, 4, 12, 20)
+STORE_TILES = (8, 8, 8, 6, 4, 4, 2)
+OUT_BUFS = 4
 SHARED_EVERY = 7
 SHARED_PHASE = 3
 
@@ -38,7 +38,7 @@ def tile_clusternorm1dv3_t_e_kernel(
     with ExitStack() as ctx:
         ctx.enter_context(tc.manual_schedule())
         const = ctx.enter_context(tc.tile_pool(name="const", bufs=1))
-        x_pool = ctx.enter_context(tc.tile_pool(name="x", bufs=N_RUNS // LOAD_RUNS))
+        x_pool = ctx.enter_context(tc.tile_pool(name="x", bufs=1))
         grouped_pool = ctx.enter_context(tc.tile_pool(name="grouped", bufs=4))
         raw_pool = ctx.enter_context(tc.tile_pool(name="raw", bufs=2))
         quant_pool = ctx.enter_context(tc.tile_pool(name="quant", bufs=6))
@@ -52,19 +52,16 @@ def tile_clusternorm1dv3_t_e_kernel(
         mu_sb = const.tile([P, PACK * CLUSTERS], BF16)
         nc.sync.dma_start(out=mu_sb[:], in_=mu_track.rearrange("(p t) c -> p (t c)", t=PACK))
 
-        x_blocks = []
-        for block in range(N_RUNS // LOAD_RUNS):
-            x_sb = x_pool.tile([P, LOAD_RUNS * RUN, ROW], BF16)
-            x_blocks.append(x_sb)
+        x_sb = x_pool.tile([P, N_TILES, ROW], BF16)
 
-        def load_runs(first_run, n_runs):
-            first = (first_run % LOAD_RUNS) * RUN
+        def load_piece(i):
+            first = sum(LOAD_TILES[:i])
             nc.sync.dma_start(
-                out=x_blocks[first_run // LOAD_RUNS][:, first : first + n_runs * RUN, :],
-                in_=x_rows[:, first_run * RUN : (first_run + n_runs) * RUN, :],
+                out=x_sb[:, first : first + LOAD_TILES[i], :],
+                in_=x_rows[:, first : first + LOAD_TILES[i], :],
             )
 
-        load_runs(0, 1)
+        load_piece(0)
 
         w_scales = const.tile([P, CLUSTERS, FEAT], U8, align_bytes=64)
         nc.vector.memset(w_scales[:].bitcast(I32), 0)
@@ -82,10 +79,8 @@ def tile_clusternorm1dv3_t_e_kernel(
             out=w_codes[:].bitcast(I32),
             in_=Std_inv_track_words.rearrange("c p d t -> p c (d t)").bitcast(I32),
         )
-        for r in range(1, LOAD_RUNS):
-            load_runs(r, 1)
-        for r in range(LOAD_RUNS, N_RUNS, LOAD_RUNS):
-            load_runs(r, LOAD_RUNS)
+        for i in range(1, len(LOAD_TILES)):
+            load_piece(i)
 
         mu_spread = (
             mu_sb[:]
@@ -108,7 +103,7 @@ def tile_clusternorm1dv3_t_e_kernel(
 
         def transpose_run(r):
             for j in range(r * RUN, (r + 1) * RUN):
-                words = x_blocks[r // LOAD_RUNS][:, j % (LOAD_RUNS * RUN), :].bitcast(F32)
+                words = x_sb[:, j, :].bitcast(F32)
                 xt = xt_pool.tile([P, PACK, P], F32)
                 for t in range(PACK):
                     nc.tensor.transpose(xt[:, t, :], words[:, t:FEAT:PACK], ident[:])
@@ -148,13 +143,14 @@ def tile_clusternorm1dv3_t_e_kernel(
             quant_of[j] = (codes, scales)
 
         def multiply_run(r):
-            block = r // STORE_RUNS
-            if r % STORE_RUNS == 0:
-                out_new = out_pool.tile([P, STORE_RUNS * RUN, ROW], F32)
+            block = [i for i in range(len(STORE_TILES)) if sum(STORE_TILES[: i + 1]) > r * RUN][0]
+            first_tile = sum(STORE_TILES[:block])
+            if r * RUN == first_tile:
+                out_new = out_pool.tile([P, STORE_TILES[block], ROW], F32)
                 out_of[block] = out_new
             out_sb = out_of[block]
             for j in range(r * RUN, (r + 1) * RUN):
-                row = j % (STORE_RUNS * RUN)
+                row = j - first_tile
                 codes, scales = quant_of[j]
                 for half in range(FEAT // D_HALF):
                     d_cols = slice(half * D_HALF, (half + 1) * D_HALF)
@@ -176,16 +172,9 @@ def tile_clusternorm1dv3_t_e_kernel(
                         ].rearrange("p (d c) -> p d c", c=CLUSTERS),
                         in_=acc[:].rearrange("p c d -> p d c"),
                     )
-            if block == N_RUNS // STORE_RUNS - 1:
-                first = (r % STORE_RUNS) * RUN
+            if (r + 1) * RUN == first_tile + STORE_TILES[block]:
                 nc.sync.dma_start(
-                    out=out_rows[:, r * RUN : (r + 1) * RUN, :],
-                    in_=out_sb[:, first : first + RUN, :],
-                )
-            elif r % STORE_RUNS == STORE_RUNS - 1:
-                nc.sync.dma_start(
-                    out=out_rows[:, block * STORE_RUNS * RUN : (block + 1) * STORE_RUNS * RUN, :],
-                    in_=out_sb[:],
+                    out=out_rows[:, first_tile : first_tile + STORE_TILES[block], :], in_=out_sb[:]
                 )
 
         transpose_run(0)

@@ -19,7 +19,7 @@ RUN = 2
 N_RUNS = N_TILES // RUN
 D_HALF = FEAT // 2
 SCALE_ROWS = 4
-LOAD_TILES = (2, 2, 4, 12, 20)
+LOAD_TILES = (2, 2, 4, 8, 8, 16)
 STORE_TILES = (8, 8, 8, 6, 4, 4, 2)
 OUT_BUFS = 4
 SHARED_EVERY = 7

@@ -49,9 +49,6 @@ def tile_clusternorm1dv3_t_e_kernel(
         ident = const.tile([P, P], F32)
         make_identity(nc, ident[:])
 
-        mu_sb = const.tile([P, PACK * CLUSTERS], BF16)
-        nc.sync.dma_start(out=mu_sb[:], in_=mu_track.rearrange("(p t) c -> p (t c)", t=PACK))
-
         x_sb = x_pool.tile([P, N_TILES, ROW], BF16)
 
         def load_piece(i):
@@ -62,6 +59,16 @@ def tile_clusternorm1dv3_t_e_kernel(
             )
 
         load_piece(0)
+
+        mu_sb = const.tile([P, PACK * CLUSTERS], BF16)
+        nc.sync.dma_start(out=mu_sb[:], in_=mu_track.rearrange("(p t) c -> p (t c)", t=PACK))
+
+        w_codes = const.tile([P, CLUSTERS, FEAT], U32, align_bytes=64)
+        nc.sync.dma_start(
+            out=w_codes[:].bitcast(I32),
+            in_=Std_inv_track_words.rearrange("c p d t -> p c (d t)").bitcast(I32),
+        )
+        load_piece(1)
 
         w_scales = const.tile([P, CLUSTERS, FEAT], U8, align_bytes=64)
         nc.vector.memset(w_scales[:].bitcast(I32), 0)
@@ -74,12 +81,7 @@ def tile_clusternorm1dv3_t_e_kernel(
                 .rearrange("c q d -> q c d")
                 .bitcast(I32),
             )
-        w_codes = const.tile([P, CLUSTERS, FEAT], U32, align_bytes=64)
-        nc.sync.dma_start(
-            out=w_codes[:].bitcast(I32),
-            in_=Std_inv_track_words.rearrange("c p d t -> p c (d t)").bitcast(I32),
-        )
-        for i in range(1, len(LOAD_TILES)):
+        for i in range(2, len(LOAD_TILES)):
             load_piece(i)
 
         mu_spread = (

@@ -49,7 +49,7 @@ def tile_clusternorm1dv3_t_e_kernel(
         ident = const.tile([P, P], F32)
         make_identity(nc, ident[:])
 
-        x_sb = x_pool.tile([P, N_TILES, ROW], BF16)
+        x_sb = x_pool.tile([P, N_TILES, ROW], BF16, align_bytes=256)
 
         def load_piece(i):
             first = sum(LOAD_TILES[:i])
@@ -63,7 +63,7 @@ def tile_clusternorm1dv3_t_e_kernel(
         mu_sb = const.tile([P, PACK * CLUSTERS], BF16)
         nc.sync.dma_start(out=mu_sb[:], in_=mu_track.rearrange("(p t) c -> p (t c)", t=PACK))
 
-        w_codes = const.tile([P, CLUSTERS, FEAT], U32, align_bytes=64)
+        w_codes = const.tile([P, CLUSTERS, FEAT], U32, align_bytes=256)
         nc.sync.dma_start(
             out=w_codes[:].bitcast(I32),
             in_=Std_inv_track_words.rearrange("c p d t -> p c (d t)").bitcast(I32),
@@ -148,7 +148,7 @@ def tile_clusternorm1dv3_t_e_kernel(
             block = [i for i in range(len(STORE_TILES)) if sum(STORE_TILES[: i + 1]) > r * RUN][0]
             first_tile = sum(STORE_TILES[:block])
             if r * RUN == first_tile:
-                out_new = out_pool.tile([P, STORE_TILES[block], ROW], F32)
+                out_new = out_pool.tile([P, STORE_TILES[block], ROW], F32, align_bytes=256)
                 out_of[block] = out_new
             out_sb = out_of[block]
             for j in range(r * RUN, (r + 1) * RUN):

@@ -20,7 +20,7 @@ N_RUNS = N_TILES // RUN
 D_HALF = FEAT // 2
 SCALE_ROWS = 4
 LOAD_TILES = (2, 2, 4, 8, 8, 16)
-STORE_TILES = (8, 8, 8, 6, 4, 4, 2)
+STORE_TILES = (10, 8, 8, 6, 6, 2)
 OUT_BUFS = 4
 SHARED_EVERY = 7
 SHARED_PHASE = 3
@@ -42,7 +42,7 @@ def tile_clusternorm1dv3_t_e_kernel(
         grouped_pool = ctx.enter_context(tc.tile_pool(name="grouped", bufs=4))
         raw_pool = ctx.enter_context(tc.tile_pool(name="raw", bufs=2))
         quant_pool = ctx.enter_context(tc.tile_pool(name="quant", bufs=6))
-        out_pool = ctx.enter_context(tc.tile_pool(name="out", bufs=OUT_BUFS))
+        out_pool = ctx.enter_context(tc.tile_pool(name="out", bufs=1))
         xt_pool = ctx.enter_context(tc.psum_pool(name="xt", bufs=2 * RUN))
         acc_pool = ctx.enter_context(tc.psum_pool(name="acc", bufs=2 * RUN))
 
@@ -61,7 +61,7 @@ def tile_clusternorm1dv3_t_e_kernel(
         load_piece(0)
 
         mu_sb = const.tile([P, PACK * CLUSTERS], BF16)
-        nc.sync.dma_start(out=mu_sb[:], in_=mu_track.rearrange("(p t) c -> p (t c)", t=PACK))
+        nc.scalar.dma_start(out=mu_sb[:], in_=mu_track.rearrange("(p t) c -> p (t c)", t=PACK))
 
         w_codes = const.tile([P, CLUSTERS, FEAT], U32, align_bytes=256)
         nc.sync.dma_start(
@@ -148,7 +148,12 @@ def tile_clusternorm1dv3_t_e_kernel(
             block = [i for i in range(len(STORE_TILES)) if sum(STORE_TILES[: i + 1]) > r * RUN][0]
             first_tile = sum(STORE_TILES[:block])
             if r * RUN == first_tile:
-                out_new = out_pool.tile([P, STORE_TILES[block], ROW], F32, align_bytes=256)
+                out_new = out_pool.tile(
+                    [P, STORE_TILES[block], ROW],
+                    F32,
+                    align_bytes=256,
+                    name=f"out_{block % OUT_BUFS}",
+                )
                 out_of[block] = out_new
             out_sb = out_of[block]
             for j in range(r * RUN, (r + 1) * RUN):

@@ -19,9 +19,9 @@ RUN = 2
 N_RUNS = N_TILES // RUN
 D_HALF = FEAT // 2
 SCALE_ROWS = 4
-LOAD_TILES = (2, 2, 4, 8, 8, 16)
+LOAD_TILES = (2, 4, 6, 12, 16)
 STORE_TILES = (10, 8, 8, 6, 6, 2)
-OUT_BUFS = 4
+OUT_BUFS = 3
 SHARED_EVERY = 7
 SHARED_PHASE = 3
 
@@ -63,12 +63,13 @@ def tile_clusternorm1dv3_t_e_kernel(
         mu_sb = const.tile([P, PACK * CLUSTERS], BF16)
         nc.scalar.dma_start(out=mu_sb[:], in_=mu_track.rearrange("(p t) c -> p (t c)", t=PACK))
 
+        load_piece(1)
+
         w_codes = const.tile([P, CLUSTERS, FEAT], U32, align_bytes=256)
         nc.sync.dma_start(
             out=w_codes[:].bitcast(I32),
             in_=Std_inv_track_words.rearrange("c p d t -> p c (d t)").bitcast(I32),
         )
-        load_piece(1)
 
         w_scales = const.tile([P, CLUSTERS, FEAT], U8, align_bytes=64)
         nc.vector.memset(w_scales[:].bitcast(I32), 0)

@@ -20,7 +20,7 @@ N_RUNS = N_TILES // RUN
 D_HALF = FEAT // 2
 SCALE_ROWS = 4
 LOAD_TILES = (2, 4, 6, 12, 16)
-STORE_TILES = (10, 8, 8, 6, 6, 2)
+STORE_TILES = (10, 8, 8, 6, 4, 4)
 OUT_BUFS = 3
 SHARED_EVERY = 7
 SHARED_PHASE = 3

@@ -20,8 +20,8 @@ N_RUNS = N_TILES // RUN
 D_HALF = FEAT // 2
 SCALE_ROWS = 4
 LOAD_TILES = (2, 4, 6, 12, 16)
-STORE_TILES = (10, 8, 8, 6, 4, 4)
-OUT_BUFS = 3
+STORE_TILES = (10, 8, 7, 6, 5, 4)
+OUT_BUFS = 4
 SHARED_EVERY = 7
 SHARED_PHASE = 3
 
@@ -146,18 +146,18 @@ def tile_clusternorm1dv3_t_e_kernel(
             quant_of[j] = (codes, scales)
 
         def multiply_run(r):
-            block = [i for i in range(len(STORE_TILES)) if sum(STORE_TILES[: i + 1]) > r * RUN][0]
-            first_tile = sum(STORE_TILES[:block])
-            if r * RUN == first_tile:
-                out_new = out_pool.tile(
-                    [P, STORE_TILES[block], ROW],
-                    F32,
-                    align_bytes=256,
-                    name=f"out_{block % OUT_BUFS}",
-                )
-                out_of[block] = out_new
-            out_sb = out_of[block]
             for j in range(r * RUN, (r + 1) * RUN):
+                block = [i for i in range(len(STORE_TILES)) if sum(STORE_TILES[: i + 1]) > j][0]
+                first_tile = sum(STORE_TILES[:block])
+                if j == first_tile:
+                    out_new = out_pool.tile(
+                        [P, STORE_TILES[block], ROW],
+                        F32,
+                        align_bytes=256,
+                        name=f"out_{block % OUT_BUFS}",
+                    )
+                    out_of[block] = out_new
+                out_sb = out_of[block]
                 row = j - first_tile
                 codes, scales = quant_of[j]
                 for half in range(FEAT // D_HALF):
@@ -180,10 +180,11 @@ def tile_clusternorm1dv3_t_e_kernel(
                         ].rearrange("p (d c) -> p d c", c=CLUSTERS),
                         in_=acc[:].rearrange("p c d -> p d c"),
                     )
-            if (r + 1) * RUN == first_tile + STORE_TILES[block]:
-                nc.sync.dma_start(
-                    out=out_rows[:, first_tile : first_tile + STORE_TILES[block], :], in_=out_sb[:]
-                )
+                if j + 1 == first_tile + STORE_TILES[block]:
+                    nc.sync.dma_start(
+                        out=out_rows[:, first_tile : first_tile + STORE_TILES[block], :],
+                        in_=out_sb[:],
+                    )
 
         transpose_run(0)
         for r in range(N_RUNS + 1):

from contextlib import ExitStack

import concourse.mybir as mybir
from concourse.masks import make_identity

F32 = mybir.dt.float32
BF16 = mybir.dt.bfloat16
I32 = mybir.dt.int32
U32 = mybir.dt.uint32
U8 = mybir.dt.uint8
FP8X4 = mybir.dt.float8_e4m3fn_x4

P = 128
PACK = 4
BATCH, FEAT, CLUSTERS = 5120, 512, 2
ROW = FEAT * CLUSTERS
N_TILES = BATCH // P
RUN = 2
N_RUNS = N_TILES // RUN
D_HALF = FEAT // 2
SCALE_ROWS = 4
LOAD_TILES = (2, 4, 6, 12, 16)
STORE_TILES = (10, 8, 7, 6, 5, 4)
OUT_BUFS = 4
SHARED_EVERY = 7
SHARED_PHASE = 3

FLOPS = 2 * BATCH * FEAT * FEAT * CLUSTERS


def tile_clusternorm1dv3_t_e_kernel(
    tc, x, mu_track, Std_inv_track_words, Std_inv_track_scales, out
):
    nc = tc.nc
    x_rows = x.rearrange("(p j) e c -> p j (e c)", j=N_TILES)
    out_rows = out.rearrange("(p j) d c -> p j (d c)", j=N_TILES)

    with ExitStack() as ctx:
        ctx.enter_context(tc.manual_schedule())
        const = ctx.enter_context(tc.tile_pool(name="const", bufs=1))
        x_pool = ctx.enter_context(tc.tile_pool(name="x", bufs=1))
        grouped_pool = ctx.enter_context(tc.tile_pool(name="grouped", bufs=4))
        raw_pool = ctx.enter_context(tc.tile_pool(name="raw", bufs=2))
        quant_pool = ctx.enter_context(tc.tile_pool(name="quant", bufs=6))
        out_pool = ctx.enter_context(tc.tile_pool(name="out", bufs=1))
        xt_pool = ctx.enter_context(tc.psum_pool(name="xt", bufs=2 * RUN))
        acc_pool = ctx.enter_context(tc.psum_pool(name="acc", bufs=2 * RUN))

        ident = const.tile([P, P], F32)
        make_identity(nc, ident[:])

        x_sb = x_pool.tile([P, N_TILES, ROW], BF16, align_bytes=256)

        def load_piece(i):
            first = sum(LOAD_TILES[:i])
            nc.sync.dma_start(
                out=x_sb[:, first : first + LOAD_TILES[i], :],
                in_=x_rows[:, first : first + LOAD_TILES[i], :],
            )

        load_piece(0)

        mu_sb = const.tile([P, PACK * CLUSTERS], BF16)
        nc.scalar.dma_start(out=mu_sb[:], in_=mu_track.rearrange("(p t) c -> p (t c)", t=PACK))

        load_piece(1)

        w_codes = const.tile([P, CLUSTERS, FEAT], U32, align_bytes=256)
        nc.sync.dma_start(
            out=w_codes[:].bitcast(I32),
            in_=Std_inv_track_words.rearrange("c p d t -> p c (d t)").bitcast(I32),
        )

        w_scales = const.tile([P, CLUSTERS, FEAT], U8, align_bytes=64)
        nc.vector.memset(w_scales[:].bitcast(I32), 0)
        for quadrant in range(P // 32):
            nc.sync.dma_start(
                out=w_scales[32 * quadrant : 32 * quadrant + SCALE_ROWS, :, :].bitcast(I32),
                in_=Std_inv_track_scales[
                    :, SCALE_ROWS * quadrant : SCALE_ROWS * (quadrant + 1), :
                ]
                .rearrange("c q d -> q c d")
                .bitcast(I32),
            )
        for i in range(2, len(LOAD_TILES)):
            load_piece(i)

        mu_spread = (
            mu_sb[:]
            .rearrange("p (t c) -> p c t", c=CLUSTERS)
            .unsqueeze(2)
            .to_broadcast([P, CLUSTERS, P, PACK])
        )

        mu_full = const.tile([P, CLUSTERS, P, PACK], BF16)
        nc.vector.tensor_copy(out=mu_full[:], in_=mu_spread)

        def shared(j):
            return j % SHARED_EVERY == SHARED_PHASE

        raw_of = {}
        xt_of = {}
        grouped_of = {}
        quant_of = {}
        out_of = {}

        def transpose_run(r):
            for j in range(r * RUN, (r + 1) * RUN):
                words = x_sb[:, j, :].bitcast(F32)
                xt = xt_pool.tile([P, PACK, P], F32)
                for t in range(PACK):
                    nc.tensor.transpose(xt[:, t, :], words[:, t:FEAT:PACK], ident[:])
                xt_of[j] = xt
                if shared(j):
                    raw = raw_pool.tile([P, CLUSTERS, P, PACK], BF16)
                    nc.scalar.copy(
                        out=raw[:],
                        in_=xt[:].bitcast(BF16).rearrange("p t (b c) -> p c b t", c=CLUSTERS),
                    )
                    raw_of[j] = raw

        def centre(j):
            grouped = grouped_pool.tile([P, CLUSTERS, P, PACK], BF16, align_bytes=64)
            if shared(j):
                nc.vector.tensor_tensor(
                    out=grouped[:], in0=raw_of[j][:], in1=mu_full[:], op=mybir.AluOpType.subtract
                )
            else:
                nc.vector.tensor_tensor(
                    out=grouped[:],
                    in0=xt_of[j][:].bitcast(BF16).rearrange("p t (b c) -> p c b t", c=CLUSTERS),
                    in1=mu_spread,
                    op=mybir.AluOpType.subtract,
                )
            grouped_of[j] = grouped

        def quantise(j):
            grouped = grouped_of[j]
            codes = quant_pool.tile([P, CLUSTERS * P], U32, align_bytes=64)
            scales = quant_pool.tile([P, CLUSTERS * P], U8, align_bytes=64)
            nc.vector.quantize_mx(
                out=codes[:].bitcast(FP8X4),
                scales=scales[:],
                in_=grouped[:].rearrange("p c b t -> p (c b t)"),
            )
            quant_of[j] = (codes, scales)

        def multiply_run(r):
            for j in range(r * RUN, (r + 1) * RUN):
                block = [i for i in range(len(STORE_TILES)) if sum(STORE_TILES[: i + 1]) > j][0]
                first_tile = sum(STORE_TILES[:block])
                if j == first_tile:
                    out_new = out_pool.tile(
                        [P, STORE_TILES[block], ROW],
                        F32,
                        align_bytes=256,
                        name=f"out_{block % OUT_BUFS}",
                    )
                    out_of[block] = out_new
                out_sb = out_of[block]
                row = j - first_tile
                codes, scales = quant_of[j]
                for half in range(FEAT // D_HALF):
                    d_cols = slice(half * D_HALF, (half + 1) * D_HALF)
                    acc = acc_pool.tile([P, CLUSTERS, D_HALF], F32)
                    for c in range(CLUSTERS):
                        b_cols = slice(c * P, (c + 1) * P)
                        nc.tensor.matmul_mx(
                            out=acc[:, c, :],
                            lhsT=codes[:, b_cols].bitcast(FP8X4),
                            lhsT_scale=scales[:, b_cols],
                            rhs=w_codes[:, c, d_cols].bitcast(FP8X4),
                            rhs_scale=w_scales[:, c, d_cols],
                            start=True,
                            stop=True,
                        )
                    nc.scalar.copy(
                        out=out_sb[
                            :, row, half * D_HALF * CLUSTERS : (half + 1) * D_HALF * CLUSTERS
                        ].rearrange("p (d c) -> p d c", c=CLUSTERS),
                        in_=acc[:].rearrange("p c d -> p d c"),
                    )
                if j + 1 == first_tile + STORE_TILES[block]:
                    nc.sync.dma_start(
                        out=out_rows[:, first_tile : first_tile + STORE_TILES[block], :],
                        in_=out_sb[:],
                    )

        transpose_run(0)
        for r in range(N_RUNS + 1):
            if r + 1 < N_RUNS:
                transpose_run(r + 1)
            for j in range(r * RUN, (r + 1) * RUN):
                if j < N_TILES:
                    centre(j)
                if 0 <= j - 1 < N_TILES:
                    quantise(j - 1)
            if r >= 1:
                multiply_run(r - 1)
